import numpy as np
import ml_dtypes


def mxq(x, axis, fmt="e4m3"):
    dtype, down = {"e4m3": (ml_dtypes.float8_e4m3fn, 7), "e5m2": (ml_dtypes.float8_e5m2, 14)}[fmt]
    v = np.moveaxis(np.asarray(x, np.float32).astype(ml_dtypes.bfloat16).astype(np.float64), axis, -1)
    blocks = v.reshape(v.shape[:-1] + (-1, 32))
    amax = np.abs(blocks).max(-1, keepdims=True)
    byte = np.maximum(np.where(amax > 0, np.frexp(amax)[1] - 1 + 127, 0) - down, 1)
    scale = np.exp2(byte - 127.0)
    codes = (blocks / scale).astype(np.float32).astype(dtype).astype(np.float64)
    return np.moveaxis((codes * scale).reshape(v.shape), -1, axis)


WIDE = False


def mx_kscale(k):
    if not WIDE:
        return np.ones(k)
    levels = np.array([30, -30])
    if k % 512:
        return np.exp2(np.random.permutation(np.resize(levels, k // 32))).repeat(32)
    a = np.empty((k // 512, 16))
    for p in range(k // 512):
        a[p, :8] = np.random.permutation(np.resize(levels, 8))
        for g in range(8):
            far = levels[np.abs(levels - a[p, g]) >= 10]
            a[p, g + 8] = far[np.random.randint(len(far))]
    return np.exp2(a.ravel()).repeat(32)


BF16 = ml_dtypes.bfloat16


def bf(x):
    return np.asarray(x, np.float32).astype(BF16)


def f64(x):
    return np.asarray(x).astype(np.float64)


B, L, D, H, QK, V = 4, 512, 1024, 8, 128, 128


def rotate_by_i(x):
    x2 = x.reshape(x.shape[:-1] + (-1, 2))
    real, imag = x2[..., 0], x2[..., 1]
    return np.stack([-imag, real], axis=-1).reshape(x.shape)


def setup_inputs():
    s = mx_kscale(D)
    a = np.random.uniform(-np.pi, np.pi, (B, L, QK // 2))
    return {"sequence": bf(np.random.standard_normal((B, L, D)) * s),
            "w_q": bf(np.random.standard_normal((H, D, QK)) * 0.3 / np.sqrt(D) / s[:, None]),
            "w_k": bf(np.random.standard_normal((H, D, QK)) * 0.3 / np.sqrt(D) / s[:, None]),
            "cos_half": bf(np.cos(a)), "sin_half": bf(np.sin(a))}


def reference(sequence, w_q, w_k, cos_half, sin_half):
    xq = mxq(f64(sequence), 2, "e5m2")[None]
    q = xq @ mxq(f64(w_q), 1, "e5m2")[:, None]
    k = xq @ mxq(f64(w_k), 1, "e5m2")[:, None]
    cos = np.repeat(f64(cos_half), 2, axis=-1)
    sin = np.repeat(f64(sin_half), 2, axis=-1)
    q_rot = cos * q + sin * rotate_by_i(q)
    k_rot = cos * k - sin * rotate_by_i(k)
    return q_rot, k_rot

@@ -1,0 +1,189 @@
+from contextlib import ExitStack
+
+import concourse.mybir as mybir
+from concourse.masks import make_identity
+
+FLOPS = 2 * 2048 * 1024 * 2048
+
+F32 = mybir.dt.float32
+BF16 = mybir.dt.bfloat16
+U32 = mybir.dt.uint32
+U8 = mybir.dt.uint8
+E5 = mybir.dt.float8_e5m2_x4
+MULT = mybir.AluOpType.mult
+ADD = mybir.AluOpType.add
+SUB = mybir.AluOpType.subtract
+
+P = 128
+NB = 4
+NJ = 4
+K = 1024
+KP = 2
+NH = 8
+NQK = 2
+C = 128
+NG = 4
+CG = 32
+IL = 16
+
+
+def tile_multiscaleretention_pa_kernel(tc, sequence, w_q, w_k, cos_half, sin_half, out_0, out_1):
+    nc = tc.nc
+    outs = (out_0, out_1)
+    weights = (w_q, w_k)
+    shape4 = [P, NQK * NH, IL, 2]
+
+    with ExitStack() as ctx:
+        keep = ctx.enter_context(tc.tile_pool(name="keep", bufs=1))
+        xgp = ctx.enter_context(tc.tile_pool(name="xgp", bufs=2))
+        xt_ps = ctx.enter_context(tc.psum_pool(name="xt_ps", bufs=2))
+        acc_ps = ctx.enter_context(tc.psum_pool(name="acc_ps", bufs=6))
+
+        ident = keep.tile([P, P], F32, name="ident")
+        make_identity(nc, ident[:])
+        warm = keep.tile([P, 1], F32, name="warm")
+        nc.scalar.copy(out=warm[:], in_=ident[:, 0:1])
+
+        xraw = [keep.tile([P, NJ, K], BF16, name="xraw%d" % s) for s in range(NB)]
+        cos_b = keep.tile([P, NB, NJ * 64], BF16, name="cos_b")
+        sin_b = keep.tile([P, NB, NJ * 64], BF16, name="sin_b")
+        tsin = keep.tile([P, NB * NJ * NG, 2, IL], BF16, name="tsin")
+        xc = keep.tile([P, NB, NJ * KP * P], U32, name="xc", align_bytes=64)
+        xs = keep.tile([P, NB, NJ * KP * P], U8, name="xs", align_bytes=64)
+        wc = keep.tile([P, KP, NG, 512], U32, name="wc", align_bytes=64)
+        ws = keep.tile([P, KP, NG, 512], U8, name="ws", align_bytes=64)
+
+        xg_of = {}
+
+        def turn(s, j):
+            if j == 0:
+                xg_new = xgp.tile([P, NJ, KP * P * 4], BF16, name="xg", align_bytes=64)
+                xg_of[s] = xg_new
+            words = xraw[s][:, j, :].bitcast(F32)
+            xt = xt_ps.tile([P, KP, 2, P], F32, name="xt")
+            for kp in range(KP):
+                for u in range(2):
+                    nc.tensor.transpose(xt[:, kp, u, :], words[:, 256 * kp + u: 256 * (kp + 1): 2], ident[:])
+            nc.scalar.copy(
+                out=xg_of[s][:, j, :].bitcast(F32).rearrange("p (k r u) -> p k r u", k=KP, u=2),
+                in_=xt[:].rearrange("p k u r -> p k r u"),
+            )
+
+        def quantize_x(s, j0, j1):
+            cols = slice(j0 * KP * P, j1 * KP * P)
+            nc.vector.quantize_mx(
+                out=xc[:, s, cols].bitcast(E5),
+                scales=xs[:, s, cols],
+                in_=xg_of[s][:, j0:j1, :].rearrange("p j n -> p (j n)"),
+            )
+
+        with tc.tile_pool(name="head", bufs=1) as head:
+            wraw = [head.tile([P, NQK, NH, NJ * C], BF16, name="wraw%d" % kp) for kp in range(KP)]
+
+            x0 = sequence[0].rearrange("(p j) k -> p j k", j=NJ)
+            nc.sync.dma_start(out=xraw[0][:, 0, :], in_=x0[:, 0, :])
+
+            def load_w(kp, qk):
+                nc.sync.dma_start(
+                    out=wraw[kp][:, qk, :, :],
+                    in_=weights[qk][:, 512 * kp: 512 * (kp + 1), :].rearrange("h (p j) c -> p h (j c)", j=NJ),
+                )
+
+            load_w(0, 0)
+            load_w(0, 1)
+            nc.sync.dma_start(out=cos_b[:], in_=cos_half.rearrange("b (p j) i -> p b (j i)", j=NJ))
+            nc.sync.dma_start(out=sin_b[:], in_=sin_half.rearrange("b (p j) i -> p b (j i)", j=NJ))
+            load_w(1, 0)
+            load_w(1, 1)
+            for j in range(1, NJ):
+                nc.sync.dma_start(out=xraw[0][:, j, :], in_=x0[:, j, :])
+            for s in range(1, NB):
+                nc.sync.dma_start(
+                    out=xraw[s][:].rearrange("p j k -> p (j k)"),
+                    in_=sequence[s].rearrange("(p j) k -> p (j k)", j=NJ),
+                )
+
+            turn(0, 0)
+            quantize_x(0, 0, 1)
+
+            sin_rows = sin_b[:].rearrange("p b (n i) -> p (b n) i", i=IL)
+            nc.vector.tensor_scalar_mul(out=tsin[:, :, 0, :], in0=sin_rows, scalar1=-1.0)
+            nc.vector.tensor_copy(out=tsin[:, :, 1, :], in_=sin_rows)
+
+            for kp in range(KP):
+                wgs = [head.tile([P, NQK, NH, CG, NJ], BF16, name="wg%d_%d" % (kp, g), align_bytes=64) for g in range(NG)]
+                for qk in range(NQK):
+                    rows = wraw[kp][:, qk, :, :].rearrange("p h (j c) -> p h j c", j=NJ)
+                    for g in range(NG):
+                        src = rows[:, :, :, CG * g: CG * (g + 1)].rearrange("p h j c -> p h c j")
+                        if g < 2:
+                            nc.vector.tensor_copy(out=wgs[g][:, qk, :, :, :], in_=src)
+                        else:
+                            nc.scalar.copy(out=wgs[g][:, qk, :, :, :], in_=src)
+                for g in range(NG):
+                    nc.vector.quantize_mx(
+                        out=wc[:, kp, g, :].bitcast(E5),
+                        scales=ws[:, kp, g, :],
+                        in_=wgs[g][:].rearrange("p q h c j -> p (q h c j)"),
+                    )
+
+            for j in range(1, NJ):
+                turn(0, j)
+                quantize_x(0, j, j + 1)
+
+        zp = ctx.enter_context(tc.tile_pool(name="zp", bufs=2))
+        rp = ctx.enter_context(tc.tile_pool(name="rp", bufs=2))
+
+        cos_rows = cos_b[:].rearrange("p b (n i) -> p (b n) i", i=IL)
+
+        r_of = {}
+        for n in range(NB * NJ):
+            s, j = n // NJ, n % NJ
+            if s + 1 < NB:
+                if j < 2:
+                    turn(s + 1, 2 * j)
+                    turn(s + 1, 2 * j + 1)
+                elif j == 2:
+                    quantize_x(s + 1, 0, NJ)
+            if j == 0:
+                r_new = rp.tile([P, NQK, NH, NJ, C], F32, name="r")
+                r_of[s] = r_new
+            r = r_of[s]
+
+            za = zp.tile([P, NQK * NH, C], F32, name="za")
+            zb = zp.tile([P, NQK * NH, C], F32, name="zb")
+            for g in range(NG):
+                acc = acc_ps.tile([P, 512], F32, name="acc")
+                for kp in range(KP):
+                    cols = slice((j * KP + kp) * P, (j * KP + kp + 1) * P)
+                    nc.tensor.matmul_mx(
+                        out=acc[:],
+                        lhsT=xc[:, s, cols].bitcast(E5),
+                        lhsT_scale=xs[:, s, cols],
+                        rhs=wc[:, kp, g, :].bitcast(E5),
+                        rhs_scale=ws[:, kp, g, :],
+                        start=(kp == 0),
+                        stop=(kp == KP - 1),
+                    )
+                chans = slice(CG * g, CG * (g + 1))
+                q4 = acc[:].rearrange("p (a i e) -> p a i e", i=IL, e=2)
+                cos4 = cos_rows[:, n * NG + g, :].unsqueeze(1).unsqueeze(3).to_broadcast(shape4)
+                sin4 = tsin[:, n * NG + g, :, :].rearrange("p e i -> p i e").unsqueeze(1).to_broadcast(shape4)
+                nc.vector.tensor_tensor(out=za[:, :, chans].rearrange("p a (i e) -> p a i e", e=2), in0=q4, in1=cos4, op=MULT)
+                nc.vector.tensor_tensor(out=zb[:, :, chans].rearrange("p a (i e) -> p a i e", e=2), in0=q4[:, :, :, ::-1], in1=sin4, op=MULT)
+            nc.gpsimd.tensor_tensor(out=r[:, 0, :, j, :], in0=za[:, 0:NH, :], in1=zb[:, 0:NH, :], op=ADD)
+            nc.gpsimd.tensor_tensor(out=r[:, 1, :, j, :], in0=za[:, NH:2 * NH, :], in1=zb[:, NH:2 * NH, :], op=SUB)
+
+            if s < NB - 1:
+                if j == NJ - 1:
+                    for qk in range(NQK):
+                        nc.sync.dma_start(
+                            out=outs[qk][:, s].rearrange("h (p j) c -> p h (j c)", j=NJ),
+                            in_=r[:, qk].rearrange("p h j c -> p h (j c)"),
+                        )
+            else:
+                for qk in range(NQK):
+                    nc.sync.dma_start(
+                        out=outs[qk][:, s].rearrange("h (p j) c -> p h j c", j=NJ)[:, :, j, :],
+                        in_=r[:, qk, :, j, :],
+                    )

@@ -13,14 +13,17 @@ E5 = mybir.dt.float8_e5m2_x4
 MULT = mybir.AluOpType.mult
 ADD = mybir.AluOpType.add
 SUB = mybir.AluOpType.subtract
+COPY = mybir.ActivationFunctionType.Copy
 
 P = 128
 NB = 4
 NJ = 4
+NT = NB * NJ
 K = 1024
 KP = 2
 NH = 8
 NQK = 2
+NA = NQK * NH
 C = 128
 NG = 4
 CG = 32
@@ -31,7 +34,6 @@ def tile_multiscaleretention_pa_kernel(tc, sequence, w_q, w_k, cos_half, sin_hal
     nc = tc.nc
     outs = (out_0, out_1)
     weights = (w_q, w_k)
-    shape4 = [P, NQK * NH, IL, 2]
 
     with ExitStack() as ctx:
         keep = ctx.enter_context(tc.tile_pool(name="keep", bufs=1))
@@ -42,12 +44,13 @@ def tile_multiscaleretention_pa_kernel(tc, sequence, w_q, w_k, cos_half, sin_hal
         ident = keep.tile([P, P], F32, name="ident")
         make_identity(nc, ident[:])
         warm = keep.tile([P, 1], F32, name="warm")
-        nc.scalar.copy(out=warm[:], in_=ident[:, 0:1])
+        nc.scalar.activation(out=warm[:], in_=ident[:, 0:1], func=COPY, scale=ident[:, 0:1])
 
         xraw = [keep.tile([P, NJ, K], BF16, name="xraw%d" % s) for s in range(NB)]
         cos_b = keep.tile([P, NB, NJ * 64], BF16, name="cos_b")
         sin_b = keep.tile([P, NB, NJ * 64], BF16, name="sin_b")
-        tsin = keep.tile([P, NB * NJ * NG, 2, IL], BF16, name="tsin")
+        cos_f = keep.tile([P, NB, NJ * 64], F32, name="cos_f")
+        tsin = keep.tile([P, NT * NG, 2, IL], BF16, name="tsin")
         xc = keep.tile([P, NB, NJ * KP * P], U32, name="xc", align_bytes=64)
         xs = keep.tile([P, NB, NJ * KP * P], U8, name="xs", align_bytes=64)
         wc = keep.tile([P, KP, NG, 512], U32, name="wc", align_bytes=64)
@@ -55,7 +58,7 @@ def tile_multiscaleretention_pa_kernel(tc, sequence, w_q, w_k, cos_half, sin_hal
 
         xg_of = {}
 
-        def turn(s, j):
+        def turn(s, j, on_vector):
             if j == 0:
                 xg_new = xgp.tile([P, NJ, KP * P * 4], BF16, name="xg", align_bytes=64)
                 xg_of[s] = xg_new
@@ -64,10 +67,11 @@ def tile_multiscaleretention_pa_kernel(tc, sequence, w_q, w_k, cos_half, sin_hal
             for kp in range(KP):
                 for u in range(2):
                     nc.tensor.transpose(xt[:, kp, u, :], words[:, 256 * kp + u: 256 * (kp + 1): 2], ident[:])
-            nc.scalar.copy(
-                out=xg_of[s][:, j, :].bitcast(F32).rearrange("p (k r u) -> p k r u", k=KP, u=2),
-                in_=xt[:].rearrange("p k u r -> p k r u"),
-            )
+            grouped = xg_of[s][:, j, :].bitcast(F32).rearrange("p (k r u) -> p k r u", k=KP, u=2)
+            if on_vector:
+                nc.vector.tensor_copy(out=grouped, in_=xt[:].rearrange("p k u r -> p k r u"))
+            else:
+                nc.scalar.copy(out=grouped, in_=xt[:].rearrange("p k u r -> p k r u"))
 
         def quantize_x(s, j0, j1):
             cols = slice(j0 * KP * P, j1 * KP * P)
@@ -77,81 +81,83 @@ def tile_multiscaleretention_pa_kernel(tc, sequence, w_q, w_k, cos_half, sin_hal
                 in_=xg_of[s][:, j0:j1, :].rearrange("p j n -> p (j n)"),
             )
 
+        def tables(b0, b1):
+            rows = slice(b0 * NJ * NG, b1 * NJ * NG)
+            sin_rows = sin_b[:, b0:b1, :].rearrange("p b (n i) -> p (b n) i", i=IL)
+            nc.vector.tensor_scalar_mul(out=tsin[:, rows, 0, :], in0=sin_rows, scalar1=-1.0)
+            nc.vector.tensor_copy(out=tsin[:, rows, 1, :], in_=sin_rows)
+            nc.gpsimd.tensor_scalar(
+                out=cos_f[:, b0:b1, :], in0=cos_b[:, b0:b1, :], scalar1=1.0, scalar2=0.0, op0=MULT, op1=ADD
+            )
+
         with tc.tile_pool(name="head", bufs=1) as head:
             wraw = [head.tile([P, NQK, NH, NJ * C], BF16, name="wraw%d" % kp) for kp in range(KP)]
 
             x0 = sequence[0].rearrange("(p j) k -> p j k", j=NJ)
             nc.sync.dma_start(out=xraw[0][:, 0, :], in_=x0[:, 0, :])
-
-            def load_w(kp, qk):
-                nc.sync.dma_start(
-                    out=wraw[kp][:, qk, :, :],
-                    in_=weights[qk][:, 512 * kp: 512 * (kp + 1), :].rearrange("h (p j) c -> p h (j c)", j=NJ),
-                )
-
-            load_w(0, 0)
-            load_w(0, 1)
-            nc.sync.dma_start(out=cos_b[:], in_=cos_half.rearrange("b (p j) i -> p b (j i)", j=NJ))
-            nc.sync.dma_start(out=sin_b[:], in_=sin_half.rearrange("b (p j) i -> p b (j i)", j=NJ))
-            load_w(1, 0)
-            load_w(1, 1)
+            nc.sync.dma_start(out=cos_b[:, 0, :], in_=cos_half[0].rearrange("(p j) i -> p (j i)", j=NJ))
+            nc.sync.dma_start(out=sin_b[:, 0, :], in_=sin_half[0].rearrange("(p j) i -> p (j i)", j=NJ))
+            for kp in range(KP):
+                for qk in range(NQK):
+                    nc.sync.dma_start(
+                        out=wraw[kp][:, qk, :, :],
+                        in_=weights[qk][:, 512 * kp: 512 * (kp + 1), :].rearrange("h (p j) c -> p h (j c)", j=NJ),
+                    )
             for j in range(1, NJ):
                 nc.sync.dma_start(out=xraw[0][:, j, :], in_=x0[:, j, :])
+            nc.sync.dma_start(out=cos_b[:, 1:NB, :], in_=cos_half[1:NB].rearrange("b (p j) i -> p b (j i)", j=NJ))
+            nc.sync.dma_start(out=sin_b[:, 1:NB, :], in_=sin_half[1:NB].rearrange("b (p j) i -> p b (j i)", j=NJ))
             for s in range(1, NB):
                 nc.sync.dma_start(
                     out=xraw[s][:].rearrange("p j k -> p (j k)"),
                     in_=sequence[s].rearrange("(p j) k -> p (j k)", j=NJ),
                 )
 
-            turn(0, 0)
+            turn(0, 0, False)
             quantize_x(0, 0, 1)
-
-            sin_rows = sin_b[:].rearrange("p b (n i) -> p (b n) i", i=IL)
-            nc.vector.tensor_scalar_mul(out=tsin[:, :, 0, :], in0=sin_rows, scalar1=-1.0)
-            nc.vector.tensor_copy(out=tsin[:, :, 1, :], in_=sin_rows)
+            tables(0, 1)
 
             for kp in range(KP):
                 wgs = [head.tile([P, NQK, NH, CG, NJ], BF16, name="wg%d_%d" % (kp, g), align_bytes=64) for g in range(NG)]
-                for qk in range(NQK):
+
+                def spread(qk, g):
                     rows = wraw[kp][:, qk, :, :].rearrange("p h (j c) -> p h j c", j=NJ)
-                    for g in range(NG):
-                        src = rows[:, :, :, CG * g: CG * (g + 1)].rearrange("p h j c -> p h c j")
-                        if g < 2:
-                            nc.vector.tensor_copy(out=wgs[g][:, qk, :, :, :], in_=src)
-                        else:
-                            nc.scalar.copy(out=wgs[g][:, qk, :, :, :], in_=src)
-                for g in range(NG):
+                    src = rows[:, :, :, CG * g: CG * (g + 1)].rearrange("p h j c -> p h c j")
+                    if g % 2 == 0:
+                        nc.vector.tensor_copy(out=wgs[g][:, qk, :, :, :], in_=src)
+                    else:
+                        nc.scalar.copy(out=wgs[g][:, qk, :, :, :], in_=src)
+
+                def quantize_w(g):
                     nc.vector.quantize_mx(
                         out=wc[:, kp, g, :].bitcast(E5),
                         scales=ws[:, kp, g, :],
                         in_=wgs[g][:].rearrange("p q h c j -> p (q h c j)"),
                     )
 
-            for j in range(1, NJ):
-                turn(0, j)
-                quantize_x(0, j, j + 1)
+                for g in range(NG):
+                    spread(0, g)
+                spread(1, 0)
+                spread(1, 1)
+                quantize_w(0)
+                spread(1, 2)
+                spread(1, 3)
+                quantize_w(1)
+                quantize_w(2)
+                quantize_w(3)
 
-        zp = ctx.enter_context(tc.tile_pool(name="zp", bufs=2))
+        zp = ctx.enter_context(tc.tile_pool(name="zp", bufs=3))
         rp = ctx.enter_context(tc.tile_pool(name="rp", bufs=2))
 
-        cos_rows = cos_b[:].rearrange("p b (n i) -> p (b n) i", i=IL)
-
+        cos_cols = cos_f[:].rearrange("p b n -> p (b n)")
+        acc_of = {}
+        zs_of = {}
+        zb_of = {}
         r_of = {}
-        for n in range(NB * NJ):
-            s, j = n // NJ, n % NJ
-            if s + 1 < NB:
-                if j < 2:
-                    turn(s + 1, 2 * j)
-                    turn(s + 1, 2 * j + 1)
-                elif j == 2:
-                    quantize_x(s + 1, 0, NJ)
-            if j == 0:
-                r_new = rp.tile([P, NQK, NH, NJ, C], F32, name="r")
-                r_of[s] = r_new
-            r = r_of[s]
 
-            za = zp.tile([P, NQK * NH, C], F32, name="za")
-            zb = zp.tile([P, NQK * NH, C], F32, name="zb")
+        def project(n):
+            s, j = n // NJ, n % NJ
+            banks = []
             for g in range(NG):
                 acc = acc_ps.tile([P, 512], F32, name="acc")
                 for kp in range(KP):
@@ -165,15 +171,40 @@ def tile_multiscaleretention_pa_kernel(tc, sequence, w_q, w_k, cos_half, sin_hal
                         start=(kp == 0),
                         stop=(kp == KP - 1),
                     )
-                chans = slice(CG * g, CG * (g + 1))
-                q4 = acc[:].rearrange("p (a i e) -> p a i e", i=IL, e=2)
-                cos4 = cos_rows[:, n * NG + g, :].unsqueeze(1).unsqueeze(3).to_broadcast(shape4)
-                sin4 = tsin[:, n * NG + g, :, :].rearrange("p e i -> p i e").unsqueeze(1).to_broadcast(shape4)
-                nc.vector.tensor_tensor(out=za[:, :, chans].rearrange("p a (i e) -> p a i e", e=2), in0=q4, in1=cos4, op=MULT)
-                nc.vector.tensor_tensor(out=zb[:, :, chans].rearrange("p a (i e) -> p a i e", e=2), in0=q4[:, :, :, ::-1], in1=sin4, op=MULT)
-            nc.gpsimd.tensor_tensor(out=r[:, 0, :, j, :], in0=za[:, 0:NH, :], in1=zb[:, 0:NH, :], op=ADD)
-            nc.gpsimd.tensor_tensor(out=r[:, 1, :, j, :], in0=za[:, NH:2 * NH, :], in1=zb[:, NH:2 * NH, :], op=SUB)
+                banks.append(acc)
+            acc_of[n] = banks
 
+        def cosine_part(n, g):
+            q4 = acc_of[n][g][:].rearrange("p (a i e) -> p a i e", i=IL, e=2)
+            for i in range(IL):
+                col = n * 64 + g * IL + i
+                nc.scalar.activation(
+                    out=zs_of[n][:, g * IL + i, :, :], in_=q4[:, :, i, :], func=COPY, scale=cos_cols[:, col:col + 1]
+                )
+
+        def sine_part(n, g):
+            q4 = acc_of[n][g][:].rearrange("p (a i e) -> p a i e", i=IL, e=2)
+            sin4 = tsin[:, n * NG + g, :, :].rearrange("p e i -> p i e").unsqueeze(1).to_broadcast([P, NA, IL, 2])
+            nc.vector.tensor_tensor(
+                out=zb_of[n][:, :, CG * g: CG * (g + 1)].rearrange("p a (i e) -> p a i e", e=2),
+                in0=q4[:, :, :, ::-1],
+                in1=sin4,
+                op=MULT,
+            )
+
+        def join(engine, n, qk, g0, g1):
+            s, j = n // NJ, n % NJ
+            heads = slice(qk * NH, (qk + 1) * NH)
+            engine.tensor_tensor(
+                out=r_of[s][:, qk, :, j, CG * g0: CG * g1].rearrange("p h (i e) -> p h i e", e=2),
+                in0=zs_of[n][:, IL * g0: IL * g1, heads, :].rearrange("p i h e -> p h i e"),
+                in1=zb_of[n][:, heads, CG * g0: CG * g1].rearrange("p h (i e) -> p h i e", e=2),
+                op=(ADD if qk == 0 else SUB),
+            )
+
+        def store(n):
+            s, j = n // NJ, n % NJ
+            r = r_of[s]
             if s < NB - 1:
                 if j == NJ - 1:
                     for qk in range(NQK):
@@ -187,3 +218,36 @@ def tile_multiscaleretention_pa_kernel(tc, sequence, w_q, w_k, cos_half, sin_hal
                         out=outs[qk][:, s].rearrange("h (p j) c -> p h j c", j=NJ)[:, :, j, :],
                         in_=r[:, qk, :, j, :],
                     )
+
+        for n in range(NT):
+            s, j = n // NJ, n % NJ
+            if j == 0:
+                r_new = rp.tile([P, NQK, NH, NJ, C], F32, name="r")
+                r_of[s] = r_new
+            zs_new = zp.tile([P, NG * IL, NA, 2], F32, name="zs")
+            zs_of[n] = zs_new
+            zb_new = zp.tile([P, NA, C], F32, name="zb")
+            zb_of[n] = zb_new
+
+            project(n)
+            if s == 0 and j + 1 < NJ:
+                turn(0, j + 1, True)
+                quantize_x(0, j + 1, j + 2)
+            if s + 1 < NB:
+                if j == 1 or j == 2:
+                    turn(s + 1, 2 * j - 2, True)
+                    turn(s + 1, 2 * j - 1, False)
+                elif j == 3:
+                    quantize_x(s + 1, 0, NJ)
+            if n == 1:
+                tables(1, NB)
+            for g in range(NG):
+                cosine_part(n, g)
+                sine_part(n, g)
+                join(nc.gpsimd, n, 0, g, g + 1)
+                if n == NT - 1:
+                    join(nc.vector, n, 1, g, g + 1)
+            if n > 0:
+                join(nc.vector, n - 1, 1, 0, NG)
+                store(n - 1)
+        store(NT - 1)

@@ -28,6 +28,7 @@ C = 128
 NG = 4
 CG = 32
 IL = 16
+NS = 3
 
 
 def tile_multiscaleretention_pa_kernel(tc, sequence, w_q, w_k, cos_half, sin_half, out_0, out_1):
@@ -150,6 +151,8 @@ def tile_multiscaleretention_pa_kernel(tc, sequence, w_q, w_k, cos_half, sin_hal
         rp = ctx.enter_context(tc.tile_pool(name="rp", bufs=2))
 
         cos_cols = cos_f[:].rearrange("p b n -> p (b n)")
+        cos_rows = cos_b[:].rearrange("p b (n i) -> p (b n) i", i=IL)
+        za_of = {}
         acc_of = {}
         zs_of = {}
         zb_of = {}
@@ -192,15 +195,33 @@ def tile_multiscaleretention_pa_kernel(tc, sequence, w_q, w_k, cos_half, sin_hal
                 op=MULT,
             )
 
+        def cosine_long(n, g):
+            q4 = acc_of[n][g][:].rearrange("p (a i e) -> p a i e", i=IL, e=2)
+            cos4 = cos_rows[:, n * NG + g, :].unsqueeze(1).unsqueeze(3).to_broadcast([P, NA, IL, 2])
+            nc.vector.tensor_tensor(
+                out=za_of[n][:, :, CG * (g - NS): CG * (g - NS + 1)].rearrange("p a (i e) -> p a i e", e=2),
+                in0=q4,
+                in1=cos4,
+                op=MULT,
+            )
+
         def join(engine, n, qk, g0, g1):
             s, j = n // NJ, n % NJ
             heads = slice(qk * NH, (qk + 1) * NH)
-            engine.tensor_tensor(
-                out=r_of[s][:, qk, :, j, CG * g0: CG * g1].rearrange("p h (i e) -> p h i e", e=2),
-                in0=zs_of[n][:, IL * g0: IL * g1, heads, :].rearrange("p i h e -> p h i e"),
-                in1=zb_of[n][:, heads, CG * g0: CG * g1].rearrange("p h (i e) -> p h i e", e=2),
-                op=(ADD if qk == 0 else SUB),
-            )
+            if g0 < NS:
+                engine.tensor_tensor(
+                    out=r_of[s][:, qk, :, j, CG * g0: CG * g1].rearrange("p h (i e) -> p h i e", e=2),
+                    in0=zs_of[n][:, IL * g0: IL * g1, heads, :].rearrange("p i h e -> p h i e"),
+                    in1=zb_of[n][:, heads, CG * g0: CG * g1].rearrange("p h (i e) -> p h i e", e=2),
+                    op=(ADD if qk == 0 else SUB),
+                )
+            else:
+                engine.tensor_tensor(
+                    out=r_of[s][:, qk, :, j, CG * g0: CG * g1],
+                    in0=za_of[n][:, heads, CG * (g0 - NS): CG * (g1 - NS)],
+                    in1=zb_of[n][:, heads, CG * g0: CG * g1],
+                    op=(ADD if qk == 0 else SUB),
+                )
 
         def store(n):
             s, j = n // NJ, n % NJ
@@ -224,8 +245,10 @@ def tile_multiscaleretention_pa_kernel(tc, sequence, w_q, w_k, cos_half, sin_hal
             if j == 0:
                 r_new = rp.tile([P, NQK, NH, NJ, C], F32, name="r")
                 r_of[s] = r_new
-            zs_new = zp.tile([P, NG * IL, NA, 2], F32, name="zs")
+            zs_new = zp.tile([P, NS * IL, NA, 2], F32, name="zs")
             zs_of[n] = zs_new
+            za_new = zp.tile([P, NA, (NG - NS) * CG], F32, name="za")
+            za_of[n] = za_new
             zb_new = zp.tile([P, NA, C], F32, name="zb")
             zb_of[n] = zb_new
 
@@ -234,20 +257,25 @@ def tile_multiscaleretention_pa_kernel(tc, sequence, w_q, w_k, cos_half, sin_hal
                 turn(0, j + 1, True)
                 quantize_x(0, j + 1, j + 2)
             if s + 1 < NB:
-                if j == 1 or j == 2:
-                    turn(s + 1, 2 * j - 2, True)
-                    turn(s + 1, 2 * j - 1, False)
-                elif j == 3:
+                turn(s + 1, j, False)
+                if j == NJ - 1:
                     quantize_x(s + 1, 0, NJ)
             if n == 1:
                 tables(1, NB)
             for g in range(NG):
-                cosine_part(n, g)
                 sine_part(n, g)
-                join(nc.gpsimd, n, 0, g, g + 1)
-                if n == NT - 1:
-                    join(nc.vector, n, 1, g, g + 1)
+                if g < NS:
+                    cosine_part(n, g)
+                    join(nc.gpsimd, n, 0, g, g + 1)
+                else:
+                    cosine_long(n, g)
+                    join(nc.gpsimd, n, 0, g, g + 1)
+                    if n < NT - 1:
+                        join(nc.gpsimd, n, 1, g, g + 1)
+                    else:
+                        join(nc.vector, n, 1, g, g + 1)
             if n > 0:
-                join(nc.vector, n - 1, 1, 0, NG)
+                join(nc.vector, n - 1, 1, 0, NS)
                 store(n - 1)
+        join(nc.vector, NT - 1, 1, 0, NS)
         store(NT - 1)

@@ -13,7 +13,6 @@ E5 = mybir.dt.float8_e5m2_x4
 MULT = mybir.AluOpType.mult
 ADD = mybir.AluOpType.add
 SUB = mybir.AluOpType.subtract
-COPY = mybir.ActivationFunctionType.Copy
 
 P = 128
 NB = 4
@@ -21,14 +20,10 @@ NJ = 4
 NT = NB * NJ
 K = 1024
 KP = 2
-NH = 8
-NQK = 2
-NA = NQK * NH
 C = 128
-NG = 4
-CG = 32
-IL = 16
-NS = 3
+NI = 64
+NGR = 4
+HG = 4
 
 
 def tile_multiscaleretention_pa_kernel(tc, sequence, w_q, w_k, cos_half, sin_half, out_0, out_1):
@@ -39,27 +34,66 @@ def tile_multiscaleretention_pa_kernel(tc, sequence, w_q, w_k, cos_half, sin_hal
     with ExitStack() as ctx:
         keep = ctx.enter_context(tc.tile_pool(name="keep", bufs=1))
         xgp = ctx.enter_context(tc.tile_pool(name="xgp", bufs=2))
+        wgp = ctx.enter_context(tc.tile_pool(name="wgp", bufs=2))
+        zp = ctx.enter_context(tc.tile_pool(name="zp", bufs=3))
         xt_ps = ctx.enter_context(tc.psum_pool(name="xt_ps", bufs=2))
-        acc_ps = ctx.enter_context(tc.psum_pool(name="acc_ps", bufs=6))
+        acc_ps = ctx.enter_context(tc.psum_pool(name="acc_ps", bufs=5))
+        pj_ps = ctx.enter_context(tc.psum_pool(name="pj_ps", bufs=1))
 
         ident = keep.tile([P, P], F32, name="ident")
         make_identity(nc, ident[:])
+        minus = keep.tile([P, P], F32, name="minus")
+        nc.vector.tensor_scalar_mul(out=minus[:], in0=ident[:], scalar1=-1.0)
         warm = keep.tile([P, 1], F32, name="warm")
-        nc.scalar.activation(out=warm[:], in_=ident[:, 0:1], func=COPY, scale=ident[:, 0:1])
+        nc.scalar.copy(out=warm[:], in_=ident[:, 0:1])
 
         xraw = [keep.tile([P, NJ, K], BF16, name="xraw%d" % s) for s in range(NB)]
-        cos_b = keep.tile([P, NB, NJ * 64], BF16, name="cos_b")
-        sin_b = keep.tile([P, NB, NJ * 64], BF16, name="sin_b")
-        cos_f = keep.tile([P, NB, NJ * 64], F32, name="cos_f")
-        tsin = keep.tile([P, NT * NG, 2, IL], BF16, name="tsin")
+        wraw = [keep.tile([P, KP, HG, NJ * C], BF16, name="wraw%d" % gr) for gr in range(NGR)]
+        cos_b = keep.tile([P, NT, NI], BF16, name="cos_b")
+        sin_b = keep.tile([P, NT, NI], BF16, name="sin_b")
+        tsin = keep.tile([P, NT, 2, NI], BF16, name="tsin")
         xc = keep.tile([P, NB, NJ * KP * P], U32, name="xc", align_bytes=64)
         xs = keep.tile([P, NB, NJ * KP * P], U8, name="xs", align_bytes=64)
-        wc = keep.tile([P, KP, NG, 512], U32, name="wc", align_bytes=64)
-        ws = keep.tile([P, KP, NG, 512], U8, name="ws", align_bytes=64)
+        wc = keep.tile([P, NGR, KP * 512], U32, name="wc", align_bytes=64)
+        ws = keep.tile([P, NGR, KP * 512], U8, name="ws", align_bytes=64)
+
+        x0 = sequence[0].rearrange("(p j) k -> p j k", j=NJ)
+
+        def load_w(gr, kp):
+            h0 = HG * (gr % 2)
+            nc.sync.dma_start(
+                out=wraw[gr][:, kp, :, :],
+                in_=weights[gr // 2][h0:h0 + HG, 512 * kp: 512 * (kp + 1), :].rearrange("h (p j) c -> p h (j c)", j=NJ),
+            )
+
+        def load_tables(b0, b1):
+            for dst, src in ((cos_b, cos_half), (sin_b, sin_half)):
+                nc.sync.dma_start(
+                    out=dst[:, b0 * NJ: b1 * NJ, :].rearrange("p (b j) i -> p b (j i)", j=NJ),
+                    in_=src[b0:b1].rearrange("b (p j) i -> p b (j i)", j=NJ),
+                )
+
+        nc.sync.dma_start(out=xraw[0][:, 0, :], in_=x0[:, 0, :])
+        load_w(0, 0)
+        load_tables(0, 1)
+        load_w(0, 1)
+        for j in range(1, NJ):
+            nc.sync.dma_start(out=xraw[0][:, j, :], in_=x0[:, j, :])
+        for s in range(1, NB):
+            nc.sync.dma_start(
+                out=xraw[s][:].rearrange("p j k -> p (j k)"),
+                in_=sequence[s].rearrange("(p j) k -> p (j k)", j=NJ),
+            )
+            if s == 1:
+                load_tables(1, NB)
+        for gr in range(1, NGR):
+            for kp in range(KP):
+                load_w(gr, kp)
 
         xg_of = {}
+        wg_of = {}
 
-        def turn(s, j, on_vector):
+        def turn(s, j):
             if j == 0:
                 xg_new = xgp.tile([P, NJ, KP * P * 4], BF16, name="xg", align_bytes=64)
                 xg_of[s] = xg_new
@@ -68,11 +102,10 @@ def tile_multiscaleretention_pa_kernel(tc, sequence, w_q, w_k, cos_half, sin_hal
             for kp in range(KP):
                 for u in range(2):
                     nc.tensor.transpose(xt[:, kp, u, :], words[:, 256 * kp + u: 256 * (kp + 1): 2], ident[:])
-            grouped = xg_of[s][:, j, :].bitcast(F32).rearrange("p (k r u) -> p k r u", k=KP, u=2)
-            if on_vector:
-                nc.vector.tensor_copy(out=grouped, in_=xt[:].rearrange("p k u r -> p k r u"))
-            else:
-                nc.scalar.copy(out=grouped, in_=xt[:].rearrange("p k u r -> p k r u"))
+            nc.scalar.copy(
+                out=xg_of[s][:, j, :].bitcast(F32).rearrange("p (k r u) -> p k r u", k=KP, u=2),
+                in_=xt[:].rearrange("p k u r -> p k r u"),
+            )
 
         def quantize_x(s, j0, j1):
             cols = slice(j0 * KP * P, j1 * KP * P)
@@ -83,199 +116,115 @@ def tile_multiscaleretention_pa_kernel(tc, sequence, w_q, w_k, cos_half, sin_hal
             )
 
         def tables(b0, b1):
-            rows = slice(b0 * NJ * NG, b1 * NJ * NG)
-            sin_rows = sin_b[:, b0:b1, :].rearrange("p b (n i) -> p (b n) i", i=IL)
-            nc.vector.tensor_scalar_mul(out=tsin[:, rows, 0, :], in0=sin_rows, scalar1=-1.0)
-            nc.vector.tensor_copy(out=tsin[:, rows, 1, :], in_=sin_rows)
-            nc.gpsimd.tensor_scalar(
-                out=cos_f[:, b0:b1, :], in0=cos_b[:, b0:b1, :], scalar1=1.0, scalar2=0.0, op0=MULT, op1=ADD
-            )
+            rows = slice(b0 * NJ, b1 * NJ)
+            nc.vector.tensor_scalar_mul(out=tsin[:, rows, 0, :], in0=sin_b[:, rows, :], scalar1=-1.0)
+            nc.vector.tensor_copy(out=tsin[:, rows, 1, :], in_=sin_b[:, rows, :])
 
-        with tc.tile_pool(name="head", bufs=1) as head:
-            wraw = [head.tile([P, NQK, NH, NJ * C], BF16, name="wraw%d" % kp) for kp in range(KP)]
-
-            x0 = sequence[0].rearrange("(p j) k -> p j k", j=NJ)
-            nc.sync.dma_start(out=xraw[0][:, 0, :], in_=x0[:, 0, :])
-            nc.sync.dma_start(out=cos_b[:, 0, :], in_=cos_half[0].rearrange("(p j) i -> p (j i)", j=NJ))
-            nc.sync.dma_start(out=sin_b[:, 0, :], in_=sin_half[0].rearrange("(p j) i -> p (j i)", j=NJ))
-            for kp in range(KP):
-                for qk in range(NQK):
-                    nc.sync.dma_start(
-                        out=wraw[kp][:, qk, :, :],
-                        in_=weights[qk][:, 512 * kp: 512 * (kp + 1), :].rearrange("h (p j) c -> p h (j c)", j=NJ),
-                    )
-            for j in range(1, NJ):
-                nc.sync.dma_start(out=xraw[0][:, j, :], in_=x0[:, j, :])
-            nc.sync.dma_start(out=cos_b[:, 1:NB, :], in_=cos_half[1:NB].rearrange("b (p j) i -> p b (j i)", j=NJ))
-            nc.sync.dma_start(out=sin_b[:, 1:NB, :], in_=sin_half[1:NB].rearrange("b (p j) i -> p b (j i)", j=NJ))
-            for s in range(1, NB):
-                nc.sync.dma_start(
-                    out=xraw[s][:].rearrange("p j k -> p (j k)"),
-                    in_=sequence[s].rearrange("(p j) k -> p (j k)", j=NJ),
-                )
-
-            turn(0, 0, False)
-            quantize_x(0, 0, 1)
-            tables(0, 1)
-
-            for kp in range(KP):
-                wgs = [head.tile([P, NQK, NH, CG, NJ], BF16, name="wg%d_%d" % (kp, g), align_bytes=64) for g in range(NG)]
-
-                def spread(qk, g):
-                    rows = wraw[kp][:, qk, :, :].rearrange("p h (j c) -> p h j c", j=NJ)
-                    src = rows[:, :, :, CG * g: CG * (g + 1)].rearrange("p h j c -> p h c j")
-                    if g % 2 == 0:
-                        nc.vector.tensor_copy(out=wgs[g][:, qk, :, :, :], in_=src)
-                    else:
-                        nc.scalar.copy(out=wgs[g][:, qk, :, :, :], in_=src)
-
-                def quantize_w(g):
-                    nc.vector.quantize_mx(
-                        out=wc[:, kp, g, :].bitcast(E5),
-                        scales=ws[:, kp, g, :],
-                        in_=wgs[g][:].rearrange("p q h c j -> p (q h c j)"),
-                    )
-
-                for g in range(NG):
-                    spread(0, g)
-                spread(1, 0)
-                spread(1, 1)
-                quantize_w(0)
-                spread(1, 2)
-                spread(1, 3)
-                quantize_w(1)
-                quantize_w(2)
-                quantize_w(3)
-
-        zp = ctx.enter_context(tc.tile_pool(name="zp", bufs=3))
-        rp = ctx.enter_context(tc.tile_pool(name="rp", bufs=2))
-
-        cos_cols = cos_f[:].rearrange("p b n -> p (b n)")
-        cos_rows = cos_b[:].rearrange("p b (n i) -> p (b n) i", i=IL)
-        za_of = {}
-        acc_of = {}
-        zs_of = {}
-        zb_of = {}
-        r_of = {}
-
-        def project(n):
-            s, j = n // NJ, n % NJ
-            banks = []
-            for g in range(NG):
-                acc = acc_ps.tile([P, 512], F32, name="acc")
-                for kp in range(KP):
-                    cols = slice((j * KP + kp) * P, (j * KP + kp + 1) * P)
-                    nc.tensor.matmul_mx(
-                        out=acc[:],
-                        lhsT=xc[:, s, cols].bitcast(E5),
-                        lhsT_scale=xs[:, s, cols],
-                        rhs=wc[:, kp, g, :].bitcast(E5),
-                        rhs_scale=ws[:, kp, g, :],
-                        start=(kp == 0),
-                        stop=(kp == KP - 1),
-                    )
-                banks.append(acc)
-            acc_of[n] = banks
-
-        def cosine_part(n, g):
-            q4 = acc_of[n][g][:].rearrange("p (a i e) -> p a i e", i=IL, e=2)
-            for i in range(IL):
-                col = n * 64 + g * IL + i
-                nc.scalar.activation(
-                    out=zs_of[n][:, g * IL + i, :, :], in_=q4[:, :, i, :], func=COPY, scale=cos_cols[:, col:col + 1]
-                )
-
-        def sine_part(n, g):
-            q4 = acc_of[n][g][:].rearrange("p (a i e) -> p a i e", i=IL, e=2)
-            sin4 = tsin[:, n * NG + g, :, :].rearrange("p e i -> p i e").unsqueeze(1).to_broadcast([P, NA, IL, 2])
-            nc.vector.tensor_tensor(
-                out=zb_of[n][:, :, CG * g: CG * (g + 1)].rearrange("p a (i e) -> p a i e", e=2),
-                in0=q4[:, :, :, ::-1],
-                in1=sin4,
-                op=MULT,
-            )
-
-        def cosine_long(n, g):
-            q4 = acc_of[n][g][:].rearrange("p (a i e) -> p a i e", i=IL, e=2)
-            cos4 = cos_rows[:, n * NG + g, :].unsqueeze(1).unsqueeze(3).to_broadcast([P, NA, IL, 2])
-            nc.vector.tensor_tensor(
-                out=za_of[n][:, :, CG * (g - NS): CG * (g - NS + 1)].rearrange("p a (i e) -> p a i e", e=2),
-                in0=q4,
-                in1=cos4,
-                op=MULT,
-            )
-
-        def join(engine, n, qk, g0, g1):
-            s, j = n // NJ, n % NJ
-            heads = slice(qk * NH, (qk + 1) * NH)
-            if g0 < NS:
-                engine.tensor_tensor(
-                    out=r_of[s][:, qk, :, j, CG * g0: CG * g1].rearrange("p h (i e) -> p h i e", e=2),
-                    in0=zs_of[n][:, IL * g0: IL * g1, heads, :].rearrange("p i h e -> p h i e"),
-                    in1=zb_of[n][:, heads, CG * g0: CG * g1].rearrange("p h (i e) -> p h i e", e=2),
-                    op=(ADD if qk == 0 else SUB),
-                )
+        def spread_w(gr, kp, half, on_vector):
+            if kp == 0 and half == 0:
+                wg_new = wgp.tile([P, KP, HG, C, NJ], BF16, name="wg", align_bytes=64)
+                wg_of[gr] = wg_new
+            hs = slice(2 * half, 2 * half + 2)
+            src = wraw[gr][:, kp, hs, :].rearrange("p h (j c) -> p h c j", j=NJ)
+            if on_vector:
+                nc.vector.tensor_copy(out=wg_of[gr][:, kp, hs, :, :], in_=src)
             else:
-                engine.tensor_tensor(
-                    out=r_of[s][:, qk, :, j, CG * g0: CG * g1],
-                    in0=za_of[n][:, heads, CG * (g0 - NS): CG * (g1 - NS)],
-                    in1=zb_of[n][:, heads, CG * g0: CG * g1],
-                    op=(ADD if qk == 0 else SUB),
-                )
+                nc.scalar.copy(out=wg_of[gr][:, kp, hs, :, :], in_=src)
 
-        def store(n):
-            s, j = n // NJ, n % NJ
-            r = r_of[s]
-            if s < NB - 1:
-                if j == NJ - 1:
-                    for qk in range(NQK):
-                        nc.sync.dma_start(
-                            out=outs[qk][:, s].rearrange("h (p j) c -> p h (j c)", j=NJ),
-                            in_=r[:, qk].rearrange("p h j c -> p h (j c)"),
+        def quantize_w(gr, kp0, kp1):
+            cols = slice(kp0 * 512, kp1 * 512)
+            nc.vector.quantize_mx(
+                out=wc[:, gr, cols].bitcast(E5),
+                scales=ws[:, gr, cols],
+                in_=wg_of[gr][:, kp0:kp1].rearrange("p k h c j -> p (k h c j)"),
+            )
+
+        def project(s, j, gr):
+            acc = acc_ps.tile([P, 512], F32, name="acc")
+            for kp in range(KP):
+                cols = slice((j * KP + kp) * P, (j * KP + kp + 1) * P)
+                wcols = slice(kp * 512, (kp + 1) * 512)
+                nc.tensor.matmul_mx(
+                    out=acc[:],
+                    lhsT=xc[:, s, cols].bitcast(E5),
+                    lhsT_scale=xs[:, s, cols],
+                    rhs=wc[:, gr, wcols].bitcast(E5),
+                    rhs_scale=ws[:, gr, wcols],
+                    start=(kp == 0),
+                    stop=(kp == KP - 1),
+                )
+            return acc
+
+        turn(0, 0)
+        quantize_x(0, 0, 1)
+        spread_w(0, 0, 0, True)
+        spread_w(0, 0, 1, False)
+        tables(0, 1)
+        quantize_w(0, 0, 1)
+        spread_w(0, 1, 0, True)
+        spread_w(0, 1, 1, False)
+        quantize_w(0, 1, 2)
+
+        for gr in range(NGR):
+            qk, h0 = gr // 2, HG * (gr % 2)
+            for s in range(NB):
+                last = gr == NGR - 1 and s == NB - 1
+                za = zp.tile([P, HG, NJ, C], F32, name="za")
+                zb = zp.tile([P, HG, NJ, C], F32, name="zb")
+                r = zp.tile([P, HG, NJ, C], F32, name="r")
+                ya = zp.tile([P, HG, C], F32, name="ya")
+                yb = zp.tile([P, HG, C], F32, name="yb")
+                on_tensor = 1 if (gr > 0 or s == NB - 1) else NJ
+                for j in range(NJ):
+                    t = s * NJ + j
+                    acc = project(s, j, gr)
+                    if gr == 0:
+                        if s == 0 and j + 1 < NJ:
+                            turn(0, j + 1)
+                            quantize_x(0, j + 1, j + 2)
+                        if s + 1 < NB:
+                            if j % 2 == 0:
+                                turn(s + 1, j)
+                                turn(s + 1, j + 1)
+                            else:
+                                quantize_x(s + 1, j - 1, j + 1)
+                        if s == 1 and j == 0:
+                            tables(1, NB)
+                    if gr + 1 < NGR:
+                        if s == 1:
+                            spread_w(gr + 1, j // 2, j % 2, False)
+                        elif s == 2 and j == 0:
+                            quantize_w(gr + 1, 0, KP)
+                    q4 = acc[:].rearrange("p (h i e) -> p h i e", h=HG, e=2)
+                    cos4 = cos_b[:, t, :].unsqueeze(1).unsqueeze(3).to_broadcast([P, HG, NI, 2])
+                    sin4 = tsin[:, t, :, :].rearrange("p e i -> p i e").unsqueeze(1).to_broadcast([P, HG, NI, 2])
+                    pa = ya[:] if j == on_tensor else za[:, :, j, :]
+                    pb = yb[:] if j == on_tensor else zb[:, :, j, :]
+                    nc.vector.tensor_tensor(out=pa.rearrange("p h (i e) -> p h i e", e=2), in0=q4, in1=cos4, op=MULT)
+                    nc.vector.tensor_tensor(
+                        out=pb.rearrange("p h (i e) -> p h i e", e=2), in0=q4[:, :, :, ::-1], in1=sin4, op=MULT
+                    )
+                    if j == on_tensor:
+                        pj = pj_ps.tile([P, HG, C], F32, name="pj")
+                        flat = pj[:].rearrange("p h c -> p (h c)")
+                        nc.tensor.matmul(out=flat, lhsT=ident[:], rhs=pa.rearrange("p h c -> p (h c)"), start=True, stop=False)
+                        nc.tensor.matmul(
+                            out=flat,
+                            lhsT=(ident[:] if qk == 0 else minus[:]),
+                            rhs=pb.rearrange("p h c -> p (h c)"),
+                            start=False,
+                            stop=True,
                         )
-            else:
-                for qk in range(NQK):
-                    nc.sync.dma_start(
-                        out=outs[qk][:, s].rearrange("h (p j) c -> p h j c", j=NJ)[:, :, j, :],
-                        in_=r[:, qk, :, j, :],
-                    )
-
-        for n in range(NT):
-            s, j = n // NJ, n % NJ
-            if j == 0:
-                r_new = rp.tile([P, NQK, NH, NJ, C], F32, name="r")
-                r_of[s] = r_new
-            zs_new = zp.tile([P, NS * IL, NA, 2], F32, name="zs")
-            zs_of[n] = zs_new
-            za_new = zp.tile([P, NA, (NG - NS) * CG], F32, name="za")
-            za_of[n] = za_new
-            zb_new = zp.tile([P, NA, C], F32, name="zb")
-            zb_of[n] = zb_new
-
-            project(n)
-            if s == 0 and j + 1 < NJ:
-                turn(0, j + 1, True)
-                quantize_x(0, j + 1, j + 2)
-            if s + 1 < NB:
-                turn(s + 1, j, False)
-                if j == NJ - 1:
-                    quantize_x(s + 1, 0, NJ)
-            if n == 1:
-                tables(1, NB)
-            for g in range(NG):
-                sine_part(n, g)
-                if g < NS:
-                    cosine_part(n, g)
-                    join(nc.gpsimd, n, 0, g, g + 1)
-                else:
-                    cosine_long(n, g)
-                    join(nc.gpsimd, n, 0, g, g + 1)
-                    if n < NT - 1:
-                        join(nc.gpsimd, n, 1, g, g + 1)
+                        nc.scalar.copy(out=r[:, :, j, :], in_=pj[:])
                     else:
-                        join(nc.vector, n, 1, g, g + 1)
-            if n > 0:
-                join(nc.vector, n - 1, 1, 0, NS)
-                store(n - 1)
-        join(nc.vector, NT - 1, 1, 0, NS)
-        store(NT - 1)
+                        nc.gpsimd.tensor_tensor(out=r[:, :, j, :], in0=pa, in1=pb, op=(ADD if qk == 0 else SUB))
+                    if last:
+                        nc.sync.dma_start(
+                            out=outs[qk][h0:h0 + HG, s].rearrange("h (p j) c -> p h j c", j=NJ)[:, :, j, :],
+                            in_=r[:, :, j, :],
+                        )
+                if not last:
+                    nc.sync.dma_start(
+                        out=outs[qk][h0:h0 + HG, s].rearrange("h (p j) c -> p h (j c)", j=NJ),
+                        in_=r[:].rearrange("p h j c -> p h (j c)"),
+                    )

@@ -51,7 +51,7 @@ def tile_multiscaleretention_pa_kernel(tc, sequence, w_q, w_k, cos_half, sin_hal
         wraw = [keep.tile([P, KP, HG, NJ * C], BF16, name="wraw%d" % gr) for gr in range(NGR)]
         cos_b = keep.tile([P, NT, NI], BF16, name="cos_b")
         sin_b = keep.tile([P, NT, NI], BF16, name="sin_b")
-        tsin = keep.tile([P, NT, 2, NI], BF16, name="tsin")
+        te = keep.tile([P, NT, 2, C], BF16, name="te")
         xc = keep.tile([P, NB, NJ * KP * P], U32, name="xc", align_bytes=64)
         xs = keep.tile([P, NB, NJ * KP * P], U8, name="xs", align_bytes=64)
         wc = keep.tile([P, NGR, KP * 512], U32, name="wc", align_bytes=64)
@@ -73,10 +73,18 @@ def tile_multiscaleretention_pa_kernel(tc, sequence, w_q, w_k, cos_half, sin_hal
                     in_=src[b0:b1].rearrange("b (p j) i -> p b (j i)", j=NJ),
                 )
 
+        def load_w_pair(kp, half):
+            hs = slice(2 * half, 2 * half + 2)
+            nc.sync.dma_start(
+                out=wraw[0][:, kp, hs, :],
+                in_=w_q[hs, 512 * kp: 512 * (kp + 1), :].rearrange("h (p j) c -> p h (j c)", j=NJ),
+            )
+
         nc.sync.dma_start(out=xraw[0][:, 0, :], in_=x0[:, 0, :])
-        load_w(0, 0)
         load_tables(0, 1)
-        load_w(0, 1)
+        for kp in range(KP):
+            load_w_pair(kp, 1)
+            load_w_pair(kp, 0)
         for j in range(1, NJ):
             nc.sync.dma_start(out=xraw[0][:, j, :], in_=x0[:, j, :])
         for s in range(1, NB):
@@ -115,10 +123,19 @@ def tile_multiscaleretention_pa_kernel(tc, sequence, w_q, w_k, cos_half, sin_hal
                 in_=xg_of[s][:, j0:j1, :].rearrange("p j n -> p (j n)"),
             )
 
-        def tables(b0, b1):
-            rows = slice(b0 * NJ, b1 * NJ)
-            nc.vector.tensor_scalar_mul(out=tsin[:, rows, 0, :], in0=sin_b[:, rows, :], scalar1=-1.0)
-            nc.vector.tensor_copy(out=tsin[:, rows, 1, :], in_=sin_b[:, rows, :])
+        def tables(b, on_vector):
+            rows = slice(b * NJ, (b + 1) * NJ)
+            cos_e = te[:, rows, 0, :].rearrange("p t (i e) -> p t i e", e=2)
+            sin_e = te[:, rows, 1, :].rearrange("p t (i e) -> p t i e", e=2)
+            cos_in = cos_b[:, rows, :].unsqueeze(3).to_broadcast([P, NJ, NI, 2])
+            if on_vector:
+                nc.vector.tensor_copy(out=cos_e, in_=cos_in)
+                nc.vector.tensor_copy(out=sin_e[:, :, :, 0], in_=sin_b[:, rows, :])
+                nc.vector.tensor_scalar_mul(out=sin_e[:, :, :, 1], in0=sin_b[:, rows, :], scalar1=-1.0)
+            else:
+                nc.scalar.copy(out=cos_e, in_=cos_in)
+                nc.scalar.copy(out=sin_e[:, :, :, 0], in_=sin_b[:, rows, :])
+                nc.scalar.mul(out=sin_e[:, :, :, 1], in_=sin_b[:, rows, :], mul=-1.0)
 
         def spread_w(gr, kp, half, on_vector):
             if kp == 0 and half == 0:
@@ -157,9 +174,9 @@ def tile_multiscaleretention_pa_kernel(tc, sequence, w_q, w_k, cos_half, sin_hal
 
         turn(0, 0)
         quantize_x(0, 0, 1)
+        tables(0, True)
         spread_w(0, 0, 0, True)
         spread_w(0, 0, 1, False)
-        tables(0, 1)
         quantize_w(0, 0, 1)
         spread_w(0, 1, 0, True)
         spread_w(0, 1, 1, False)
@@ -169,8 +186,7 @@ def tile_multiscaleretention_pa_kernel(tc, sequence, w_q, w_k, cos_half, sin_hal
             qk, h0 = gr // 2, HG * (gr % 2)
             for s in range(NB):
                 last = gr == NGR - 1 and s == NB - 1
-                za = zp.tile([P, HG, NJ, C], F32, name="za")
-                zb = zp.tile([P, HG, NJ, C], F32, name="zb")
+                z = zp.tile([P, 2, HG, NJ, C], F32, name="z")
                 r = zp.tile([P, HG, NJ, C], F32, name="r")
                 ya = zp.tile([P, HG, C], F32, name="ya")
                 yb = zp.tile([P, HG, C], F32, name="yb")
@@ -188,36 +204,48 @@ def tile_multiscaleretention_pa_kernel(tc, sequence, w_q, w_k, cos_half, sin_hal
                                 turn(s + 1, j + 1)
                             else:
                                 quantize_x(s + 1, j - 1, j + 1)
-                        if s == 1 and j == 0:
-                            tables(1, NB)
+                        if s + 1 < NB and j == 2:
+                            tables(s + 1, False)
                     if gr + 1 < NGR:
                         if s == 1:
                             spread_w(gr + 1, j // 2, j % 2, False)
                         elif s == 2 and j == 0:
                             quantize_w(gr + 1, 0, KP)
-                    q4 = acc[:].rearrange("p (h i e) -> p h i e", h=HG, e=2)
-                    cos4 = cos_b[:, t, :].unsqueeze(1).unsqueeze(3).to_broadcast([P, HG, NI, 2])
-                    sin4 = tsin[:, t, :, :].rearrange("p e i -> p i e").unsqueeze(1).to_broadcast([P, HG, NI, 2])
-                    pa = ya[:] if j == on_tensor else za[:, :, j, :]
-                    pb = yb[:] if j == on_tensor else zb[:, :, j, :]
-                    nc.vector.tensor_tensor(out=pa.rearrange("p h (i e) -> p h i e", e=2), in0=q4, in1=cos4, op=MULT)
-                    nc.vector.tensor_tensor(
-                        out=pb.rearrange("p h (i e) -> p h i e", e=2), in0=q4[:, :, :, ::-1], in1=sin4, op=MULT
-                    )
+                    pairs = "p h (i e) -> p h i e"
                     if j == on_tensor:
+                        q4 = acc[:].rearrange("p (h i e) -> p h i e", h=HG, e=2)
+                        cos4 = te[:, t, 0, :].rearrange("p (i e) -> p i e", e=2).unsqueeze(1).to_broadcast([P, HG, NI, 2])
+                        sin2 = te[:, t, 1, :].rearrange("p (i e) -> p i e", e=2)[:, :, ::-1]
+                        sin4 = sin2.unsqueeze(1).to_broadcast([P, HG, NI, 2])
+                        nc.vector.tensor_tensor(out=ya[:].rearrange(pairs, e=2), in0=q4, in1=cos4, op=MULT)
+                        nc.vector.tensor_tensor(out=yb[:].rearrange(pairs, e=2), in0=q4[:, :, :, ::-1], in1=sin4, op=MULT)
                         pj = pj_ps.tile([P, HG, C], F32, name="pj")
                         flat = pj[:].rearrange("p h c -> p (h c)")
-                        nc.tensor.matmul(out=flat, lhsT=ident[:], rhs=pa.rearrange("p h c -> p (h c)"), start=True, stop=False)
+                        nc.tensor.matmul(
+                            out=flat, lhsT=ident[:], rhs=ya[:].rearrange("p h c -> p (h c)"), start=True, stop=False
+                        )
                         nc.tensor.matmul(
                             out=flat,
                             lhsT=(ident[:] if qk == 0 else minus[:]),
-                            rhs=pb.rearrange("p h c -> p (h c)"),
+                            rhs=yb[:].rearrange("p h c -> p (h c)"),
                             start=False,
                             stop=True,
                         )
                         nc.scalar.copy(out=r[:, :, j, :], in_=pj[:])
                     else:
-                        nc.gpsimd.tensor_tensor(out=r[:, :, j, :], in0=pa, in1=pb, op=(ADD if qk == 0 else SUB))
+                        nc.vector.tensor_tensor(
+                            out=z[:, :, :, j, :],
+                            in0=acc[:].rearrange("p (h c) -> p h c", h=HG).unsqueeze(1).to_broadcast([P, 2, HG, C]),
+                            in1=te[:, t, :, :].unsqueeze(2).to_broadcast([P, 2, HG, C]),
+                            op=MULT,
+                        )
+                        adder = nc.vector if (last and j == NJ - 1) else nc.gpsimd
+                        adder.tensor_tensor(
+                            out=r[:, :, j, :].rearrange(pairs, e=2),
+                            in0=z[:, 0, :, j, :].rearrange(pairs, e=2),
+                            in1=z[:, 1, :, j, :].rearrange(pairs, e=2)[:, :, :, ::-1],
+                            op=(ADD if qk == 0 else SUB),
+                        )
                     if last:
                         nc.sync.dma_start(
                             out=outs[qk][h0:h0 + HG, s].rearrange("h (p j) c -> p h j c", j=NJ)[:, :, j, :],

@@ -52,10 +52,10 @@ def tile_multiscaleretention_pa_kernel(tc, sequence, w_q, w_k, cos_half, sin_hal
         cos_b = keep.tile([P, NT, NI], BF16, name="cos_b")
         sin_b = keep.tile([P, NT, NI], BF16, name="sin_b")
         te = keep.tile([P, NT, 2, C], BF16, name="te")
-        xc = keep.tile([P, NB, NJ * KP * P], U32, name="xc", align_bytes=64)
-        xs = keep.tile([P, NB, NJ * KP * P], U8, name="xs", align_bytes=64)
-        wc = keep.tile([P, NGR, KP * 512], U32, name="wc", align_bytes=64)
-        ws = keep.tile([P, NGR, KP * 512], U8, name="ws", align_bytes=64)
+        xc = keep.tile([P, NB, NJ * KP * P], U32, name="xc", align_bytes=256)
+        xs = keep.tile([P, NB, NJ * KP * P], U8, name="xs", align_bytes=256)
+        wc = keep.tile([P, NGR, KP * 512], U32, name="wc", align_bytes=256)
+        ws = keep.tile([P, NGR, KP * 512], U8, name="ws", align_bytes=256)
 
         x0 = sequence[0].rearrange("(p j) k -> p j k", j=NJ)
 

from contextlib import ExitStack

import concourse.mybir as mybir
from concourse.masks import make_identity

FLOPS = 2 * 2048 * 1024 * 2048

F32 = mybir.dt.float32
BF16 = mybir.dt.bfloat16
U32 = mybir.dt.uint32
U8 = mybir.dt.uint8
E5 = mybir.dt.float8_e5m2_x4
MULT = mybir.AluOpType.mult
ADD = mybir.AluOpType.add
SUB = mybir.AluOpType.subtract

P = 128
NB = 4
NJ = 4
NT = NB * NJ
K = 1024
KP = 2
C = 128
NI = 64
NGR = 4
HG = 4


def tile_multiscaleretention_pa_kernel(tc, sequence, w_q, w_k, cos_half, sin_half, out_0, out_1):
    nc = tc.nc
    outs = (out_0, out_1)
    weights = (w_q, w_k)

    with ExitStack() as ctx:
        keep = ctx.enter_context(tc.tile_pool(name="keep", bufs=1))
        xgp = ctx.enter_context(tc.tile_pool(name="xgp", bufs=2))
        wgp = ctx.enter_context(tc.tile_pool(name="wgp", bufs=2))
        zp = ctx.enter_context(tc.tile_pool(name="zp", bufs=3))
        xt_ps = ctx.enter_context(tc.psum_pool(name="xt_ps", bufs=2))
        acc_ps = ctx.enter_context(tc.psum_pool(name="acc_ps", bufs=5))
        pj_ps = ctx.enter_context(tc.psum_pool(name="pj_ps", bufs=1))

        ident = keep.tile([P, P], F32, name="ident")
        make_identity(nc, ident[:])
        minus = keep.tile([P, P], F32, name="minus")
        nc.vector.tensor_scalar_mul(out=minus[:], in0=ident[:], scalar1=-1.0)
        warm = keep.tile([P, 1], F32, name="warm")
        nc.scalar.copy(out=warm[:], in_=ident[:, 0:1])

        xraw = [keep.tile([P, NJ, K], BF16, name="xraw%d" % s) for s in range(NB)]
        wraw = [keep.tile([P, KP, HG, NJ * C], BF16, name="wraw%d" % gr) for gr in range(NGR)]
        cos_b = keep.tile([P, NT, NI], BF16, name="cos_b")
        sin_b = keep.tile([P, NT, NI], BF16, name="sin_b")
        te = keep.tile([P, NT, 2, C], BF16, name="te")
        xc = keep.tile([P, NB, NJ * KP * P], U32, name="xc", align_bytes=256)
        xs = keep.tile([P, NB, NJ * KP * P], U8, name="xs", align_bytes=256)
        wc = keep.tile([P, NGR, KP * 512], U32, name="wc", align_bytes=256)
        ws = keep.tile([P, NGR, KP * 512], U8, name="ws", align_bytes=256)

        x0 = sequence[0].rearrange("(p j) k -> p j k", j=NJ)

        def load_w(gr, kp):
            h0 = HG * (gr % 2)
            nc.sync.dma_start(
                out=wraw[gr][:, kp, :, :],
                in_=weights[gr // 2][h0:h0 + HG, 512 * kp: 512 * (kp + 1), :].rearrange("h (p j) c -> p h (j c)", j=NJ),
            )

        def load_tables(b0, b1):
            for dst, src in ((cos_b, cos_half), (sin_b, sin_half)):
                nc.sync.dma_start(
                    out=dst[:, b0 * NJ: b1 * NJ, :].rearrange("p (b j) i -> p b (j i)", j=NJ),
                    in_=src[b0:b1].rearrange("b (p j) i -> p b (j i)", j=NJ),
                )

        def load_w_pair(kp, half):
            hs = slice(2 * half, 2 * half + 2)
            nc.sync.dma_start(
                out=wraw[0][:, kp, hs, :],
                in_=w_q[hs, 512 * kp: 512 * (kp + 1), :].rearrange("h (p j) c -> p h (j c)", j=NJ),
            )

        nc.sync.dma_start(out=xraw[0][:, 0, :], in_=x0[:, 0, :])
        load_tables(0, 1)
        for kp in range(KP):
            load_w_pair(kp, 1)
            load_w_pair(kp, 0)
        for j in range(1, NJ):
            nc.sync.dma_start(out=xraw[0][:, j, :], in_=x0[:, j, :])
        for s in range(1, NB):
            nc.sync.dma_start(
                out=xraw[s][:].rearrange("p j k -> p (j k)"),
                in_=sequence[s].rearrange("(p j) k -> p (j k)", j=NJ),
            )
            if s == 1:
                load_tables(1, NB)
        for gr in range(1, NGR):
            for kp in range(KP):
                load_w(gr, kp)

        xg_of = {}
        wg_of = {}

        def turn(s, j):
            if j == 0:
                xg_new = xgp.tile([P, NJ, KP * P * 4], BF16, name="xg", align_bytes=64)
                xg_of[s] = xg_new
            words = xraw[s][:, j, :].bitcast(F32)
            xt = xt_ps.tile([P, KP, 2, P], F32, name="xt")
            for kp in range(KP):
                for u in range(2):
                    nc.tensor.transpose(xt[:, kp, u, :], words[:, 256 * kp + u: 256 * (kp + 1): 2], ident[:])
            nc.scalar.copy(
                out=xg_of[s][:, j, :].bitcast(F32).rearrange("p (k r u) -> p k r u", k=KP, u=2),
                in_=xt[:].rearrange("p k u r -> p k r u"),
            )

        def quantize_x(s, j0, j1):
            cols = slice(j0 * KP * P, j1 * KP * P)
            nc.vector.quantize_mx(
                out=xc[:, s, cols].bitcast(E5),
                scales=xs[:, s, cols],
                in_=xg_of[s][:, j0:j1, :].rearrange("p j n -> p (j n)"),
            )

        def tables(b, on_vector):
            rows = slice(b * NJ, (b + 1) * NJ)
            cos_e = te[:, rows, 0, :].rearrange("p t (i e) -> p t i e", e=2)
            sin_e = te[:, rows, 1, :].rearrange("p t (i e) -> p t i e", e=2)
            cos_in = cos_b[:, rows, :].unsqueeze(3).to_broadcast([P, NJ, NI, 2])
            if on_vector:
                nc.vector.tensor_copy(out=cos_e, in_=cos_in)
                nc.vector.tensor_copy(out=sin_e[:, :, :, 0], in_=sin_b[:, rows, :])
                nc.vector.tensor_scalar_mul(out=sin_e[:, :, :, 1], in0=sin_b[:, rows, :], scalar1=-1.0)
            else:
                nc.scalar.copy(out=cos_e, in_=cos_in)
                nc.scalar.copy(out=sin_e[:, :, :, 0], in_=sin_b[:, rows, :])
                nc.scalar.mul(out=sin_e[:, :, :, 1], in_=sin_b[:, rows, :], mul=-1.0)

        def spread_w(gr, kp, half, on_vector):
            if kp == 0 and half == 0:
                wg_new = wgp.tile([P, KP, HG, C, NJ], BF16, name="wg", align_bytes=64)
                wg_of[gr] = wg_new
            hs = slice(2 * half, 2 * half + 2)
            src = wraw[gr][:, kp, hs, :].rearrange("p h (j c) -> p h c j", j=NJ)
            if on_vector:
                nc.vector.tensor_copy(out=wg_of[gr][:, kp, hs, :, :], in_=src)
            else:
                nc.scalar.copy(out=wg_of[gr][:, kp, hs, :, :], in_=src)

        def quantize_w(gr, kp0, kp1):
            cols = slice(kp0 * 512, kp1 * 512)
            nc.vector.quantize_mx(
                out=wc[:, gr, cols].bitcast(E5),
                scales=ws[:, gr, cols],
                in_=wg_of[gr][:, kp0:kp1].rearrange("p k h c j -> p (k h c j)"),
            )

        def project(s, j, gr):
            acc = acc_ps.tile([P, 512], F32, name="acc")
            for kp in range(KP):
                cols = slice((j * KP + kp) * P, (j * KP + kp + 1) * P)
                wcols = slice(kp * 512, (kp + 1) * 512)
                nc.tensor.matmul_mx(
                    out=acc[:],
                    lhsT=xc[:, s, cols].bitcast(E5),
                    lhsT_scale=xs[:, s, cols],
                    rhs=wc[:, gr, wcols].bitcast(E5),
                    rhs_scale=ws[:, gr, wcols],
                    start=(kp == 0),
                    stop=(kp == KP - 1),
                )
            return acc

        turn(0, 0)
        quantize_x(0, 0, 1)
        tables(0, True)
        spread_w(0, 0, 0, True)
        spread_w(0, 0, 1, False)
        quantize_w(0, 0, 1)
        spread_w(0, 1, 0, True)
        spread_w(0, 1, 1, False)
        quantize_w(0, 1, 2)

        for gr in range(NGR):
            qk, h0 = gr // 2, HG * (gr % 2)
            for s in range(NB):
                last = gr == NGR - 1 and s == NB - 1
                z = zp.tile([P, 2, HG, NJ, C], F32, name="z")
                r = zp.tile([P, HG, NJ, C], F32, name="r")
                ya = zp.tile([P, HG, C], F32, name="ya")
                yb = zp.tile([P, HG, C], F32, name="yb")
                on_tensor = 1 if (gr > 0 or s == NB - 1) else NJ
                for j in range(NJ):
                    t = s * NJ + j
                    acc = project(s, j, gr)
                    if gr == 0:
                        if s == 0 and j + 1 < NJ:
                            turn(0, j + 1)
                            quantize_x(0, j + 1, j + 2)
                        if s + 1 < NB:
                            if j % 2 == 0:
                                turn(s + 1, j)
                                turn(s + 1, j + 1)
                            else:
                                quantize_x(s + 1, j - 1, j + 1)
                        if s + 1 < NB and j == 2:
                            tables(s + 1, False)
                    if gr + 1 < NGR:
                        if s == 1:
                            spread_w(gr + 1, j // 2, j % 2, False)
                        elif s == 2 and j == 0:
                            quantize_w(gr + 1, 0, KP)
                    pairs = "p h (i e) -> p h i e"
                    if j == on_tensor:
                        q4 = acc[:].rearrange("p (h i e) -> p h i e", h=HG, e=2)
                        cos4 = te[:, t, 0, :].rearrange("p (i e) -> p i e", e=2).unsqueeze(1).to_broadcast([P, HG, NI, 2])
                        sin2 = te[:, t, 1, :].rearrange("p (i e) -> p i e", e=2)[:, :, ::-1]
                        sin4 = sin2.unsqueeze(1).to_broadcast([P, HG, NI, 2])
                        nc.vector.tensor_tensor(out=ya[:].rearrange(pairs, e=2), in0=q4, in1=cos4, op=MULT)
                        nc.vector.tensor_tensor(out=yb[:].rearrange(pairs, e=2), in0=q4[:, :, :, ::-1], in1=sin4, op=MULT)
                        pj = pj_ps.tile([P, HG, C], F32, name="pj")
                        flat = pj[:].rearrange("p h c -> p (h c)")
                        nc.tensor.matmul(
                            out=flat, lhsT=ident[:], rhs=ya[:].rearrange("p h c -> p (h c)"), start=True, stop=False
                        )
                        nc.tensor.matmul(
                            out=flat,
                            lhsT=(ident[:] if qk == 0 else minus[:]),
                            rhs=yb[:].rearrange("p h c -> p (h c)"),
                            start=False,
                            stop=True,
                        )
                        nc.scalar.copy(out=r[:, :, j, :], in_=pj[:])
                    else:
                        nc.vector.tensor_tensor(
                            out=z[:, :, :, j, :],
                            in0=acc[:].rearrange("p (h c) -> p h c", h=HG).unsqueeze(1).to_broadcast([P, 2, HG, C]),
                            in1=te[:, t, :, :].unsqueeze(2).to_broadcast([P, 2, HG, C]),
                            op=MULT,
                        )
                        adder = nc.vector if (last and j == NJ - 1) else nc.gpsimd
                        adder.tensor_tensor(
                            out=r[:, :, j, :].rearrange(pairs, e=2),
                            in0=z[:, 0, :, j, :].rearrange(pairs, e=2),
                            in1=z[:, 1, :, j, :].rearrange(pairs, e=2)[:, :, :, ::-1],
                            op=(ADD if qk == 0 else SUB),
                        )
                    if last:
                        nc.sync.dma_start(
                            out=outs[qk][h0:h0 + HG, s].rearrange("h (p j) c -> p h j c", j=NJ)[:, :, j, :],
                            in_=r[:, :, j, :],
                        )
                if not last:
                    nc.sync.dma_start(
                        out=outs[qk][h0:h0 + HG, s].rearrange("h (p j) c -> p h (j c)", j=NJ),
                        in_=r[:].rearrange("p h j c -> p h (j c)"),
                    )
